import numpy as np
import ml_dtypes


def mxq(x, axis, fmt="e4m3"):
    dtype, down = {"e4m3": (ml_dtypes.float8_e4m3fn, 7), "e5m2": (ml_dtypes.float8_e5m2, 14)}[fmt]
    v = np.moveaxis(np.asarray(x, np.float32).astype(ml_dtypes.bfloat16).astype(np.float64), axis, -1)
    blocks = v.reshape(v.shape[:-1] + (-1, 32))
    amax = np.abs(blocks).max(-1, keepdims=True)
    byte = np.maximum(np.where(amax > 0, np.frexp(amax)[1] - 1 + 127, 0) - down, 1)
    scale = np.exp2(byte - 127.0)
    codes = (blocks / scale).astype(np.float32).astype(dtype).astype(np.float64)
    return np.moveaxis((codes * scale).reshape(v.shape), -1, axis)


WIDE = False


def mx_kscale(k):
    if not WIDE:
        return np.ones(k)
    levels = np.array([10, -10, 5, -5, 0])
    a = np.random.permutation(np.resize(levels, k // 512 * 4)).reshape(k // 512, 4)
    idx = np.arange(k)
    return np.exp2(a[idx // 512, idx % 128 // 32])


BF16 = ml_dtypes.bfloat16


def bf(x):
    return np.asarray(x, np.float32).astype(BF16)


def f64(x):
    return np.asarray(x).astype(np.float64)


B, CIN, H, W, COUT, N = 4, 512, 16, 16, 128, 9


def setup_inputs():
    s = mx_kscale(CIN)
    return {"x": bf(np.random.standard_normal((B, CIN, H, W)) * s[None, :, None, None]),
            "weights": bf(np.random.standard_normal((N, COUT, CIN, 1, 1)) * np.sqrt(N) / np.sqrt(CIN) / s[None, None, :, None, None]),
            "biases": bf(np.random.standard_normal((N, COUT)) * 0.5 * np.sqrt(N))}


def reference(x, weights, biases):
    w = np.mean(f64(weights), axis=0)[:, :, 0, 0]
    b = np.mean(f64(biases), axis=0)
    y = np.einsum('bchw,oc->bohw', mxq(f64(x), 1, "e4m3"), mxq(w, 1, "e4m3"), optimize=True) + b[None, :, None, None]
    return y

@@ -1,0 +1,116 @@
+import concourse.mybir as mybir
+from concourse.masks import make_identity
+
+BF16 = mybir.dt.bfloat16
+F32 = mybir.dt.float32
+U32 = mybir.dt.uint32
+U8 = mybir.dt.uint8
+FP8X4 = mybir.dt.float8_e4m3fn_x4
+IDENTITY = mybir.ActivationFunctionType.Identity
+
+P = 128
+PACK = 4
+B, CIN, PIXELS, COUT, LAYERS = 4, 512, 256, 128, 9
+HALVES = 2
+PAIR = 2
+assert CIN == P * PACK and PACK == HALVES * PAIR and COUT == P
+
+FLOPS = 2 * B * PIXELS * CIN * COUT
+
+
+def tile_conv_1x1_9_layer_s_kernel(tc, x, weights, biases, out):
+    nc = tc.nc
+    with tc.tile_pool(name="keep", bufs=1) as keep, tc.psum_pool(name="psum", bufs=1) as psum:
+        w_raw = keep.tile([P, LAYERS, CIN], BF16)
+        layer_groups = [(0, 2), (2, 4), (4, 6), (6, 9)]
+        for first, end in layer_groups:
+            nc.sync.dma_start(
+                out=w_raw[:, first:end, :],
+                in_=weights[first:end].rearrange("i o c a b -> o i (c a b)"),
+            )
+        x_raw = keep.tile([P, B, PACK, PIXELS], BF16)
+        for n in range(B):
+            nc.sync.dma_start(
+                out=x_raw[:, n].rearrange("p (u e) s -> p u (e s)", u=HALVES),
+                in_=x[n].rearrange("(u p e) h w -> p u (e h w)", u=HALVES, e=PAIR),
+            )
+
+        ident = keep.tile([P, P], F32)
+        make_identity(nc, ident[:])
+        bias_rows = keep.tile([P, COUT], BF16)
+        nc.vector.memset(bias_rows[:], 0.0)
+        nc.scalar.dma_start(out=bias_rows[0:LAYERS, :], in_=biases)
+        ones = keep.tile([P, 1], BF16)
+        nc.vector.memset(ones[:], 1.0)
+        bias_sum = psum.tile([P, 1], F32)
+        nc.tensor.matmul(out=bias_sum[:], lhsT=bias_rows[:], rhs=ones[:], start=True, stop=True)
+        bias_mean = keep.tile([P, 1], F32)
+        nc.scalar.mul(out=bias_mean[:], in_=bias_sum[:], mul=1.0 / LAYERS)
+
+        pair_sum = keep.tile([P, 4, CIN], F32)
+        for j in range(4):
+            nc.vector.tensor_add(
+                out=pair_sum[:, j, :], in0=w_raw[:, 2 * j, :], in1=w_raw[:, 2 * j + 1, :]
+            )
+        quad_sum = keep.tile([P, 2, CIN], F32)
+        for j in range(2):
+            nc.vector.tensor_add(
+                out=quad_sum[:, j, :], in0=pair_sum[:, 2 * j, :], in1=pair_sum[:, 2 * j + 1, :]
+            )
+        five_sum = keep.tile([P, CIN], F32)
+        nc.vector.tensor_add(out=five_sum[:], in0=quad_sum[:, 0, :], in1=w_raw[:, LAYERS - 1, :])
+        w_sum = keep.tile([P, CIN], F32)
+        nc.vector.tensor_add(out=w_sum[:], in0=five_sum[:], in1=quad_sum[:, 1, :])
+
+        w_sum_by_t = w_sum[:].rearrange("o (u p e) -> o u e p", u=HALVES, e=PAIR)
+        w_t = psum.tile([P, PACK, COUT], F32)
+        for u in range(HALVES):
+            for e in range(PAIR):
+                nc.tensor.transpose(w_t[:, PAIR * u + e, :], w_sum_by_t[:, u, e, :], ident[:])
+        w_grouped = keep.tile([P, COUT, PACK], BF16, align_bytes=64)
+        nc.vector.tensor_scalar_mul(
+            out=w_grouped[:], in0=w_t[:].rearrange("p t o -> p o t"), scalar1=1.0 / LAYERS
+        )
+        w_codes = keep.tile([P, COUT], U32, align_bytes=64)
+        w_scales = keep.tile([P, COUT], U8, align_bytes=64)
+        nc.vector.quantize_mx(
+            out=w_codes[:].bitcast(FP8X4),
+            scales=w_scales[:],
+            in_=w_grouped[:].rearrange("p o t -> p (o t)"),
+        )
+
+        x_grouped = keep.tile([P, B, PIXELS, PACK], BF16, align_bytes=64)
+        x_codes = keep.tile([P, B, PIXELS], U32, align_bytes=64)
+        x_scales = keep.tile([P, B, PIXELS], U8, align_bytes=64)
+        y_sb = keep.tile([P, B, PIXELS], F32)
+        for n in range(B):
+            grouped_view = x_grouped[:, n].rearrange("p (c i) t -> p c t i", i=4)
+            raw_view = x_raw[:, n].rearrange("p t (c i) -> p c t i", i=4)
+            if n < B - 1:
+                nc.scalar.copy(out=grouped_view, in_=raw_view)
+            else:
+                nc.vector.tensor_copy(out=grouped_view, in_=raw_view)
+        for n in range(B):
+            nc.vector.quantize_mx(
+                out=x_codes[:, n, :].bitcast(FP8X4),
+                scales=x_scales[:, n, :],
+                in_=x_grouped[:, n].rearrange("p s t -> p (s t)"),
+            )
+        for n in range(B):
+            y_ps = psum.tile([P, PIXELS], F32, name="y_ps%d" % n)
+            nc.tensor.matmul_mx(
+                out=y_ps[:],
+                lhsT=w_codes[:].bitcast(FP8X4),
+                lhsT_scale=w_scales[:],
+                rhs=x_codes[:, n, :].bitcast(FP8X4),
+                rhs_scale=x_scales[:, n, :],
+                start=True,
+                stop=True,
+            )
+            if n % 2 == 0:
+                nc.scalar.activation(
+                    out=y_sb[:, n, :], in_=y_ps[:], func=IDENTITY, bias=bias_mean[:], scale=1.0
+                )
+            else:
+                nc.vector.tensor_scalar_add(out=y_sb[:, n, :], in0=y_ps[:], scalar1=bias_mean[:])
+            nc.sync.dma_start(out=out[n].rearrange("o h w -> o (h w)"), in_=y_sb[:, n, :])

@@ -13,6 +13,8 @@ PACK = 4
 B, CIN, PIXELS, COUT, LAYERS = 4, 512, 256, 128, 9
 HALVES = 2
 PAIR = 2
+TERMS = 5
+assert LAYERS == 2 * TERMS - 1
 assert CIN == P * PACK and PACK == HALVES * PAIR and COUT == P
 
 FLOPS = 2 * B * PIXELS * CIN * COUT
@@ -22,8 +24,8 @@ def tile_conv_1x1_9_layer_s_kernel(tc, x, weights, biases, out):
     nc = tc.nc
     with tc.tile_pool(name="keep", bufs=1) as keep, tc.psum_pool(name="psum", bufs=1) as psum:
         w_raw = keep.tile([P, LAYERS, CIN], BF16)
-        layer_groups = [(0, 2), (2, 4), (4, 6), (6, 9)]
-        for first, end in layer_groups:
+        for j in range(TERMS):
+            first, end = max(2 * j - 1, 0), 2 * j + 1
             nc.sync.dma_start(
                 out=w_raw[:, first:end, :],
                 in_=weights[first:end].rearrange("i o c a b -> o i (c a b)"),
@@ -47,30 +49,28 @@ def tile_conv_1x1_9_layer_s_kernel(tc, x, weights, biases, out):
         bias_mean = keep.tile([P, 1], F32)
         nc.scalar.mul(out=bias_mean[:], in_=bias_sum[:], mul=1.0 / LAYERS)
 
-        pair_sum = keep.tile([P, 4, CIN], F32)
-        for j in range(4):
+        term = keep.tile([P, TERMS, CIN], F32)
+        nc.scalar.copy(out=term[:, 0, :], in_=w_raw[:, 0, :])
+        for j in range(1, TERMS):
             nc.vector.tensor_add(
-                out=pair_sum[:, j, :], in0=w_raw[:, 2 * j, :], in1=w_raw[:, 2 * j + 1, :]
+                out=term[:, j, :], in0=w_raw[:, 2 * j - 1, :], in1=w_raw[:, 2 * j, :]
             )
-        quad_sum = keep.tile([P, 2, CIN], F32)
-        for j in range(2):
-            nc.vector.tensor_add(
-                out=quad_sum[:, j, :], in0=pair_sum[:, 2 * j, :], in1=pair_sum[:, 2 * j + 1, :]
-            )
-        five_sum = keep.tile([P, CIN], F32)
-        nc.vector.tensor_add(out=five_sum[:], in0=quad_sum[:, 0, :], in1=w_raw[:, LAYERS - 1, :])
-        w_sum = keep.tile([P, CIN], F32)
-        nc.vector.tensor_add(out=w_sum[:], in0=five_sum[:], in1=quad_sum[:, 1, :])
-
-        w_sum_by_t = w_sum[:].rearrange("o (u p e) -> o u e p", u=HALVES, e=PAIR)
+        term_by_t = term[:].rearrange("o j (u p e) -> o j u e p", u=HALVES, e=PAIR)
         w_t = psum.tile([P, PACK, COUT], F32)
-        for u in range(HALVES):
-            for e in range(PAIR):
-                nc.tensor.transpose(w_t[:, PAIR * u + e, :], w_sum_by_t[:, u, e, :], ident[:])
+        for j in range(TERMS):
+            for u in range(HALVES):
+                for e in range(PAIR):
+                    t = PAIR * u + e
+                    nc.tensor.matmul(
+                        out=w_t[:, t, :],
+                        lhsT=term_by_t[:, j, u, e, :],
+                        rhs=ident[:],
+                        is_transpose=True,
+                        start=(j == 0 and t == 0),
+                        stop=(j == TERMS - 1 and t == PACK - 1),
+                    )
         w_grouped = keep.tile([P, COUT, PACK], BF16, align_bytes=64)
-        nc.vector.tensor_scalar_mul(
-            out=w_grouped[:], in0=w_t[:].rearrange("p t o -> p o t"), scalar1=1.0 / LAYERS
-        )
+        nc.scalar.mul(out=w_grouped[:], in_=w_t[:].rearrange("p t o -> p o t"), mul=1.0 / LAYERS)
         w_codes = keep.tile([P, COUT], U32, align_bytes=64)
         w_scales = keep.tile([P, COUT], U8, align_bytes=64)
         nc.vector.quantize_mx(
@@ -86,10 +86,9 @@ def tile_conv_1x1_9_layer_s_kernel(tc, x, weights, biases, out):
         for n in range(B):
             grouped_view = x_grouped[:, n].rearrange("p (c i) t -> p c t i", i=4)
             raw_view = x_raw[:, n].rearrange("p t (c i) -> p c t i", i=4)
-            if n < B - 1:
-                nc.scalar.copy(out=grouped_view, in_=raw_view)
-            else:
-                nc.vector.tensor_copy(out=grouped_view, in_=raw_view)
+            runs = PIXELS // 4 // 2
+            nc.vector.tensor_copy(out=grouped_view[:, :runs], in_=raw_view[:, :runs])
+            nc.scalar.copy(out=grouped_view[:, runs:], in_=raw_view[:, runs:])
         for n in range(B):
             nc.vector.quantize_mx(
                 out=x_codes[:, n, :].bitcast(FP8X4),

@@ -1,3 +1,5 @@
+from contextlib import ExitStack
+
 import concourse.mybir as mybir
 from concourse.masks import make_identity
 
@@ -22,42 +24,39 @@ FLOPS = 2 * B * PIXELS * CIN * COUT
 
 def tile_conv_1x1_9_layer_s_kernel(tc, x, weights, biases, out):
     nc = tc.nc
-    with tc.tile_pool(name="keep", bufs=1) as keep, tc.psum_pool(name="psum", bufs=1) as psum:
+    with ExitStack() as ctx:
+        keep = ctx.enter_context(tc.tile_pool(name="keep", bufs=1))
+        psum = ctx.enter_context(tc.psum_pool(name="psum", bufs=1))
+
         w_raw = keep.tile([P, LAYERS, CIN], BF16)
-        for j in range(TERMS):
+        term = keep.tile([P, TERMS, CIN], F32)
+        term_by_t = term[:].rearrange("o j (u p e) -> o j u e p", u=HALVES, e=PAIR)
+        w_t = psum.tile([P, PACK, COUT], F32)
+        x_raw = keep.tile([P, B, PACK, PIXELS], BF16)
+        x_grouped = keep.tile([P, B, PIXELS, PACK], BF16, align_bytes=64)
+        x_codes = keep.tile([P, B, PIXELS], U32, align_bytes=64)
+        x_scales = keep.tile([P, B, PIXELS], U8, align_bytes=64)
+        y_sb = keep.tile([P, B, PIXELS], F32)
+
+        def load_term(j):
             first, end = max(2 * j - 1, 0), 2 * j + 1
             nc.sync.dma_start(
                 out=w_raw[:, first:end, :],
                 in_=weights[first:end].rearrange("i o c a b -> o i (c a b)"),
             )
-        x_raw = keep.tile([P, B, PACK, PIXELS], BF16)
-        for n in range(B):
+
+        def load_image(n):
             nc.sync.dma_start(
                 out=x_raw[:, n].rearrange("p (u e) s -> p u (e s)", u=HALVES),
                 in_=x[n].rearrange("(u p e) h w -> p u (e h w)", u=HALVES, e=PAIR),
             )
 
-        ident = keep.tile([P, P], F32)
-        make_identity(nc, ident[:])
-        bias_rows = keep.tile([P, COUT], BF16)
-        nc.vector.memset(bias_rows[:], 0.0)
-        nc.scalar.dma_start(out=bias_rows[0:LAYERS, :], in_=biases)
-        ones = keep.tile([P, 1], BF16)
-        nc.vector.memset(ones[:], 1.0)
-        bias_sum = psum.tile([P, 1], F32)
-        nc.tensor.matmul(out=bias_sum[:], lhsT=bias_rows[:], rhs=ones[:], start=True, stop=True)
-        bias_mean = keep.tile([P, 1], F32)
-        nc.scalar.mul(out=bias_mean[:], in_=bias_sum[:], mul=1.0 / LAYERS)
-
-        term = keep.tile([P, TERMS, CIN], F32)
-        nc.scalar.copy(out=term[:, 0, :], in_=w_raw[:, 0, :])
-        for j in range(1, TERMS):
+        def add_term(j):
             nc.vector.tensor_add(
                 out=term[:, j, :], in0=w_raw[:, 2 * j - 1, :], in1=w_raw[:, 2 * j, :]
             )
-        term_by_t = term[:].rearrange("o j (u p e) -> o j u e p", u=HALVES, e=PAIR)
-        w_t = psum.tile([P, PACK, COUT], F32)
-        for j in range(TERMS):
+
+        def transpose_term(j):
             for u in range(HALVES):
                 for e in range(PAIR):
                     t = PAIR * u + e
@@ -69,8 +68,62 @@ def tile_conv_1x1_9_layer_s_kernel(tc, x, weights, biases, out):
                         start=(j == 0 and t == 0),
                         stop=(j == TERMS - 1 and t == PACK - 1),
                     )
+
+        def regroup_image(copy, n):
+            copy(
+                out=x_grouped[:, n].rearrange("p (c i) t -> p c t i", i=4),
+                in_=x_raw[:, n].rearrange("p t (c i) -> p c t i", i=4),
+            )
+
+        def quantise_image(n):
+            nc.vector.quantize_mx(
+                out=x_codes[:, n, :].bitcast(FP8X4),
+                scales=x_scales[:, n, :],
+                in_=x_grouped[:, n].rearrange("p s t -> p (s t)"),
+            )
+
+        load_term(0)
+        load_image(0)
+        load_term(1)
+        load_term(2)
+        load_image(1)
+        load_term(3)
+        load_term(4)
+        load_image(2)
+        load_image(3)
+
+        ident = keep.tile([P, P], F32)
+        make_identity(nc, ident[:])
+        bias_rows = keep.tile([P, COUT], BF16)
+        nc.vector.memset(bias_rows[:], 0.0)
+        nc.scalar.dma_start(out=bias_rows[0:LAYERS, :], in_=biases)
+        ones = keep.tile([P, 1], BF16)
+        nc.vector.memset(ones[:], 1.0)
+
+        nc.scalar.copy(out=term[:, 0, :], in_=w_raw[:, 0, :])
+        transpose_term(0)
+        regroup_image(nc.scalar.copy, 0)
+        add_term(1)
+        transpose_term(1)
+        add_term(2)
+        transpose_term(2)
+        quantise_image(0)
+        regroup_image(nc.scalar.copy, 1)
+        bias_sum = psum.tile([P, 1], F32)
+        nc.tensor.matmul(out=bias_sum[:], lhsT=bias_rows[:], rhs=ones[:], start=True, stop=True)
+        bias_mean = keep.tile([P, 1], F32)
+        nc.scalar.mul(out=bias_mean[:], in_=bias_sum[:], mul=1.0 / LAYERS)
+        add_term(3)
+        transpose_term(3)
+        add_term(4)
+        transpose_term(4)
+        quantise_image(1)
+
         w_grouped = keep.tile([P, COUT, PACK], BF16, align_bytes=64)
         nc.scalar.mul(out=w_grouped[:], in_=w_t[:].rearrange("p t o -> p o t"), mul=1.0 / LAYERS)
+        regroup_image(nc.vector.tensor_copy, 2)
+        regroup_image(nc.vector.tensor_copy, 3)
+        quantise_image(2)
         w_codes = keep.tile([P, COUT], U32, align_bytes=64)
         w_scales = keep.tile([P, COUT], U8, align_bytes=64)
         nc.vector.quantize_mx(
@@ -78,23 +131,8 @@ def tile_conv_1x1_9_layer_s_kernel(tc, x, weights, biases, out):
             scales=w_scales[:],
             in_=w_grouped[:].rearrange("p o t -> p (o t)"),
         )
+        quantise_image(3)
 
-        x_grouped = keep.tile([P, B, PIXELS, PACK], BF16, align_bytes=64)
-        x_codes = keep.tile([P, B, PIXELS], U32, align_bytes=64)
-        x_scales = keep.tile([P, B, PIXELS], U8, align_bytes=64)
-        y_sb = keep.tile([P, B, PIXELS], F32)
-        for n in range(B):
-            grouped_view = x_grouped[:, n].rearrange("p (c i) t -> p c t i", i=4)
-            raw_view = x_raw[:, n].rearrange("p t (c i) -> p c t i", i=4)
-            runs = PIXELS // 4 // 2
-            nc.vector.tensor_copy(out=grouped_view[:, :runs], in_=raw_view[:, :runs])
-            nc.scalar.copy(out=grouped_view[:, runs:], in_=raw_view[:, runs:])
-        for n in range(B):
-            nc.vector.quantize_mx(
-                out=x_codes[:, n, :].bitcast(FP8X4),
-                scales=x_scales[:, n, :],
-                in_=x_grouped[:, n].rearrange("p s t -> p (s t)"),
-            )
         for n in range(B):
             y_ps = psum.tile([P, PIXELS], F32, name="y_ps%d" % n)
             nc.tensor.matmul_mx(

@@ -27,6 +27,7 @@ def tile_conv_1x1_9_layer_s_kernel(tc, x, weights, biases, out):
     with ExitStack() as ctx:
         keep = ctx.enter_context(tc.tile_pool(name="keep", bufs=1))
         psum = ctx.enter_context(tc.psum_pool(name="psum", bufs=1))
+        ctx.enter_context(tc.manual_schedule())
 
         w_raw = keep.tile([P, LAYERS, CIN], BF16)
         term = keep.tile([P, TERMS, CIN], F32)

@@ -12,12 +12,13 @@ IDENTITY = mybir.ActivationFunctionType.Identity
 
 P = 128
 PACK = 4
-B, CIN, PIXELS, COUT, LAYERS = 4, 512, 256, 128, 9
 HALVES = 2
 PAIR = 2
+B, CIN, PIXELS, COUT, LAYERS = 4, 512, 256, 128, 9
 TERMS = 5
-assert LAYERS == 2 * TERMS - 1
-assert CIN == P * PACK and PACK == HALVES * PAIR and COUT == P
+RUN = 4
+VECTOR_PIXELS = 192
+assert CIN == P * PACK and PACK == HALVES * PAIR and COUT == P and LAYERS == 2 * TERMS - 1
 
 FLOPS = 2 * B * PIXELS * CIN * COUT
 
@@ -33,31 +34,42 @@ def tile_conv_1x1_9_layer_s_kernel(tc, x, weights, biases, out):
         term = keep.tile([P, TERMS, CIN], F32)
         term_by_t = term[:].rearrange("o j (u p e) -> o j u e p", u=HALVES, e=PAIR)
         w_t = psum.tile([P, PACK, COUT], F32)
+        w_grouped = keep.tile([P, COUT, PACK], BF16, align_bytes=64)
+        w_codes = keep.tile([P, COUT], U32, align_bytes=64)
+        w_scales = keep.tile([P, COUT], U8, align_bytes=64)
         x_raw = keep.tile([P, B, PACK, PIXELS], BF16)
         x_grouped = keep.tile([P, B, PIXELS, PACK], BF16, align_bytes=64)
         x_codes = keep.tile([P, B, PIXELS], U32, align_bytes=64)
         x_scales = keep.tile([P, B, PIXELS], U8, align_bytes=64)
         y_sb = keep.tile([P, B, PIXELS], F32)
 
-        def load_term(j):
+        for j in range(TERMS):
             first, end = max(2 * j - 1, 0), 2 * j + 1
             nc.sync.dma_start(
                 out=w_raw[:, first:end, :],
                 in_=weights[first:end].rearrange("i o c a b -> o i (c a b)"),
             )
-
-        def load_image(n):
+        for n in range(B):
             nc.sync.dma_start(
                 out=x_raw[:, n].rearrange("p (u e) s -> p u (e s)", u=HALVES),
                 in_=x[n].rearrange("(u p e) h w -> p u (e h w)", u=HALVES, e=PAIR),
             )
 
-        def add_term(j):
-            nc.vector.tensor_add(
-                out=term[:, j, :], in0=w_raw[:, 2 * j - 1, :], in1=w_raw[:, 2 * j, :]
-            )
+        ident = keep.tile([P, P], F32)
+        make_identity(nc, ident[:])
+        bias_rows = keep.tile([P, COUT], BF16)
+        nc.vector.memset(bias_rows[:], 0.0)
+        nc.scalar.dma_start(out=bias_rows[0:LAYERS, :], in_=biases)
+        ones = keep.tile([P, 1], BF16)
+        nc.vector.memset(ones[:], 1.0)
 
-        def transpose_term(j):
+        for j in range(TERMS):
+            if j == 0:
+                nc.scalar.copy(out=term[:, 0, :], in_=w_raw[:, 0, :])
+            else:
+                nc.vector.tensor_add(
+                    out=term[:, j, :], in0=w_raw[:, 2 * j - 1, :], in1=w_raw[:, 2 * j, :]
+                )
             for u in range(HALVES):
                 for e in range(PAIR):
                     t = PAIR * u + e
@@ -69,12 +81,15 @@ def tile_conv_1x1_9_layer_s_kernel(tc, x, weights, biases, out):
                         start=(j == 0 and t == 0),
                         stop=(j == TERMS - 1 and t == PACK - 1),
                     )
+        bias_sum = psum.tile([P, 1], F32)
+        nc.tensor.matmul(out=bias_sum[:], lhsT=bias_rows[:], rhs=ones[:], start=True, stop=True)
 
-        def regroup_image(copy, n):
-            copy(
-                out=x_grouped[:, n].rearrange("p (c i) t -> p c t i", i=4),
-                in_=x_raw[:, n].rearrange("p t (c i) -> p c t i", i=4),
-            )
+        def regroup_image(n):
+            grouped = x_grouped[:, n].rearrange("p (r i) t -> p r t i", i=RUN)
+            raw = x_raw[:, n].rearrange("p t (r i) -> p r t i", i=RUN)
+            runs = VECTOR_PIXELS // RUN
+            nc.vector.tensor_copy(out=grouped[:, :runs], in_=raw[:, :runs])
+            nc.scalar.copy(out=grouped[:, runs:], in_=raw[:, runs:])
 
         def quantise_image(n):
             nc.vector.quantize_mx(
@@ -83,55 +98,23 @@ def tile_conv_1x1_9_layer_s_kernel(tc, x, weights, biases, out):
                 in_=x_grouped[:, n].rearrange("p s t -> p (s t)"),
             )
 
-        load_term(0)
-        load_image(0)
-        load_term(1)
-        load_term(2)
-        load_image(1)
-        load_term(3)
-        load_term(4)
-        load_image(2)
-        load_image(3)
-
-        ident = keep.tile([P, P], F32)
-        make_identity(nc, ident[:])
-        bias_rows = keep.tile([P, COUT], BF16)
-        nc.vector.memset(bias_rows[:], 0.0)
-        nc.scalar.dma_start(out=bias_rows[0:LAYERS, :], in_=biases)
-        ones = keep.tile([P, 1], BF16)
-        nc.vector.memset(ones[:], 1.0)
-
-        nc.scalar.copy(out=term[:, 0, :], in_=w_raw[:, 0, :])
-        transpose_term(0)
-        regroup_image(nc.scalar.copy, 0)
-        add_term(1)
-        transpose_term(1)
-        add_term(2)
-        transpose_term(2)
+        regroup_image(0)
+        regroup_image(1)
         quantise_image(0)
-        regroup_image(nc.scalar.copy, 1)
-        bias_sum = psum.tile([P, 1], F32)
-        nc.tensor.matmul(out=bias_sum[:], lhsT=bias_rows[:], rhs=ones[:], start=True, stop=True)
-        bias_mean = keep.tile([P, 1], F32)
-        nc.scalar.mul(out=bias_mean[:], in_=bias_sum[:], mul=1.0 / LAYERS)
-        add_term(3)
-        transpose_term(3)
-        add_term(4)
-        transpose_term(4)
         quantise_image(1)
 
-        w_grouped = keep.tile([P, COUT, PACK], BF16, align_bytes=64)
         nc.scalar.mul(out=w_grouped[:], in_=w_t[:].rearrange("p t o -> p o t"), mul=1.0 / LAYERS)
-        regroup_image(nc.vector.tensor_copy, 2)
-        regroup_image(nc.vector.tensor_copy, 3)
-        quantise_image(2)
-        w_codes = keep.tile([P, COUT], U32, align_bytes=64)
-        w_scales = keep.tile([P, COUT], U8, align_bytes=64)
+        bias_mean = keep.tile([P, 1], F32)
+        nc.scalar.mul(out=bias_mean[:], in_=bias_sum[:], mul=1.0 / LAYERS)
+        regroup_image(2)
         nc.vector.quantize_mx(
             out=w_codes[:].bitcast(FP8X4),
             scales=w_scales[:],
             in_=w_grouped[:].rearrange("p o t -> p (o t)"),
         )
+
+        regroup_image(3)
+        quantise_image(2)
         quantise_image(3)
 
         for n in range(B):

@@ -12,13 +12,11 @@ IDENTITY = mybir.ActivationFunctionType.Identity
 
 P = 128
 PACK = 4
-HALVES = 2
-PAIR = 2
 B, CIN, PIXELS, COUT, LAYERS = 4, 512, 256, 128, 9
 TERMS = 5
 RUN = 4
 VECTOR_PIXELS = 192
-assert CIN == P * PACK and PACK == HALVES * PAIR and COUT == P and LAYERS == 2 * TERMS - 1
+assert CIN == P * PACK and COUT == P and LAYERS == 2 * TERMS - 1
 
 FLOPS = 2 * B * PIXELS * CIN * COUT
 
@@ -31,8 +29,8 @@ def tile_conv_1x1_9_layer_s_kernel(tc, x, weights, biases, out):
         ctx.enter_context(tc.manual_schedule())
 
         w_raw = keep.tile([P, LAYERS, CIN], BF16)
-        term = keep.tile([P, TERMS, CIN], F32)
-        term_by_t = term[:].rearrange("o j (u p e) -> o j u e p", u=HALVES, e=PAIR)
+        w_by_t = w_raw[:].rearrange("o i (p t) -> o i t p", t=PACK)
+        term = keep.tile([P, TERMS, PACK, P], F32)
         w_t = psum.tile([P, PACK, COUT], F32)
         w_grouped = keep.tile([P, COUT, PACK], BF16, align_bytes=64)
         w_codes = keep.tile([P, COUT], U32, align_bytes=64)
@@ -51,8 +49,8 @@ def tile_conv_1x1_9_layer_s_kernel(tc, x, weights, biases, out):
             )
         for n in range(B):
             nc.sync.dma_start(
-                out=x_raw[:, n].rearrange("p (u e) s -> p u (e s)", u=HALVES),
-                in_=x[n].rearrange("(u p e) h w -> p u (e h w)", u=HALVES, e=PAIR),
+                out=x_raw[:, n].rearrange("p t s -> p (t s)"),
+                in_=x[n].rearrange("(p t) h w -> p (t h w)", t=PACK),
             )
 
         ident = keep.tile([P, P], F32)
@@ -65,22 +63,18 @@ def tile_conv_1x1_9_layer_s_kernel(tc, x, weights, biases, out):
 
         for j in range(TERMS):
             if j == 0:
-                nc.scalar.copy(out=term[:, 0, :], in_=w_raw[:, 0, :])
+                nc.scalar.copy(out=term[:, 0], in_=w_by_t[:, 0])
             else:
-                nc.vector.tensor_add(
-                    out=term[:, j, :], in0=w_raw[:, 2 * j - 1, :], in1=w_raw[:, 2 * j, :]
+                nc.vector.tensor_add(out=term[:, j], in0=w_by_t[:, 2 * j - 1], in1=w_by_t[:, 2 * j])
+            for t in range(PACK):
+                nc.tensor.matmul(
+                    out=w_t[:, t, :],
+                    lhsT=term[:, j, t, :],
+                    rhs=ident[:],
+                    is_transpose=True,
+                    start=(j == 0 and t == 0),
+                    stop=(j == TERMS - 1 and t == PACK - 1),
                 )
-            for u in range(HALVES):
-                for e in range(PAIR):
-                    t = PAIR * u + e
-                    nc.tensor.matmul(
-                        out=w_t[:, t, :],
-                        lhsT=term_by_t[:, j, u, e, :],
-                        rhs=ident[:],
-                        is_transpose=True,
-                        start=(j == 0 and t == 0),
-                        stop=(j == TERMS - 1 and t == PACK - 1),
-                    )
         bias_sum = psum.tile([P, 1], F32)
         nc.tensor.matmul(out=bias_sum[:], lhsT=bias_rows[:], rhs=ones[:], start=True, stop=True)
 

@@ -14,7 +14,7 @@ P = 128
 PACK = 4
 B, CIN, PIXELS, COUT, LAYERS = 4, 512, 256, 128, 9
 TERMS = 5
-RUN = 4
+RUN = 1
 VECTOR_PIXELS = 192
 assert CIN == P * PACK and COUT == P and LAYERS == 2 * TERMS - 1
 

@@ -57,7 +57,7 @@ def tile_conv_1x1_9_layer_s_kernel(tc, x, weights, biases, out):
         make_identity(nc, ident[:])
         bias_rows = keep.tile([P, COUT], BF16)
         nc.vector.memset(bias_rows[:], 0.0)
-        nc.scalar.dma_start(out=bias_rows[0:LAYERS, :], in_=biases)
+        nc.gpsimd.dma_start(out=bias_rows[0:LAYERS, :], in_=biases)
         ones = keep.tile([P, 1], BF16)
         nc.vector.memset(ones[:], 1.0)
 

@@ -14,6 +14,7 @@ P = 128
 PACK = 4
 B, CIN, PIXELS, COUT, LAYERS = 4, 512, 256, 128, 9
 TERMS = 5
+WARM = 12
 RUN = 1
 VECTOR_PIXELS = 192
 assert CIN == P * PACK and COUT == P and LAYERS == 2 * TERMS - 1
@@ -60,6 +61,9 @@ def tile_conv_1x1_9_layer_s_kernel(tc, x, weights, biases, out):
         nc.gpsimd.dma_start(out=bias_rows[0:LAYERS, :], in_=biases)
         ones = keep.tile([P, 1], BF16)
         nc.vector.memset(ones[:], 1.0)
+        warm = psum.tile([P, P], F32)
+        for k in range(WARM):
+            nc.tensor.matmul(out=warm[:], lhsT=ident[:], rhs=ident[:], is_transpose=True, start=True, stop=True)
 
         for j in range(TERMS):
             if j == 0:

@@ -13,13 +13,12 @@ IDENTITY = mybir.ActivationFunctionType.Identity
 P = 128
 PACK = 4
 B, CIN, PIXELS, COUT, LAYERS = 4, 512, 256, 128, 9
-TERMS = 5
-WARM = 12
-RUN = 1
-VECTOR_PIXELS = 192
-assert CIN == P * PACK and COUT == P and LAYERS == 2 * TERMS - 1
+assert CIN == P * PACK and COUT == P
 
 FLOPS = 2 * B * PIXELS * CIN * COUT
+
+TERMS = 5
+WARM = 12
 
 
 def tile_conv_1x1_9_layer_s_kernel(tc, x, weights, biases, out):
@@ -41,95 +40,151 @@ def tile_conv_1x1_9_layer_s_kernel(tc, x, weights, biases, out):
         x_codes = keep.tile([P, B, PIXELS], U32, align_bytes=64)
         x_scales = keep.tile([P, B, PIXELS], U8, align_bytes=64)
         y_sb = keep.tile([P, B, PIXELS], F32)
+        ident = keep.tile([P, P], F32)
+        bias_rows = keep.tile([P, COUT], BF16)
+        ones = keep.tile([P, 1], BF16)
+        bias_sum = psum.tile([P, 1], F32)
+        bias_mean = keep.tile([P, 1], F32)
+        warm = psum.tile([P, P], F32)
+        y_ps = {}
+        passes = []
 
-        for j in range(TERMS):
-            first, end = max(2 * j - 1, 0), 2 * j + 1
+        def load_layers(first, end):
             nc.sync.dma_start(
                 out=w_raw[:, first:end, :],
                 in_=weights[first:end].rearrange("i o c a b -> o i (c a b)"),
             )
-        for n in range(B):
+
+        def load_image(n):
             nc.sync.dma_start(
                 out=x_raw[:, n].rearrange("p t s -> p (t s)"),
                 in_=x[n].rearrange("(p t) h w -> p (t h w)", t=PACK),
             )
 
-        ident = keep.tile([P, P], F32)
-        make_identity(nc, ident[:])
-        bias_rows = keep.tile([P, COUT], BF16)
-        nc.vector.memset(bias_rows[:], 0.0)
-        nc.gpsimd.dma_start(out=bias_rows[0:LAYERS, :], in_=biases)
-        ones = keep.tile([P, 1], BF16)
-        nc.vector.memset(ones[:], 1.0)
-        warm = psum.tile([P, P], F32)
-        for k in range(WARM):
-            nc.tensor.matmul(out=warm[:], lhsT=ident[:], rhs=ident[:], is_transpose=True, start=True, stop=True)
+        def idle_transposes(count):
+            for k in range(count):
+                nc.tensor.matmul(out=warm[:], lhsT=ident[:], rhs=ident[:], is_transpose=True, start=True, stop=True)
 
-        for j in range(TERMS):
-            if j == 0:
-                nc.scalar.copy(out=term[:, 0], in_=w_by_t[:, 0])
-            else:
-                nc.vector.tensor_add(out=term[:, j], in0=w_by_t[:, 2 * j - 1], in1=w_by_t[:, 2 * j])
+        def cast_layer(j, i):
+            nc.scalar.copy(out=term[:, j], in_=w_by_t[:, i])
+
+        def add_layers(j, i):
+            nc.vector.tensor_add(out=term[:, j], in0=w_by_t[:, i], in1=w_by_t[:, i + 1])
+
+        def transpose_term(j):
             for t in range(PACK):
+                passes.append(j)
                 nc.tensor.matmul(
                     out=w_t[:, t, :],
                     lhsT=term[:, j, t, :],
                     rhs=ident[:],
                     is_transpose=True,
-                    start=(j == 0 and t == 0),
-                    stop=(j == TERMS - 1 and t == PACK - 1),
+                    start=(len(passes) == 1),
+                    stop=(len(passes) == TERMS * PACK),
                 )
-        bias_sum = psum.tile([P, 1], F32)
-        nc.tensor.matmul(out=bias_sum[:], lhsT=bias_rows[:], rhs=ones[:], start=True, stop=True)
 
-        def regroup_image(n):
-            grouped = x_grouped[:, n].rearrange("p (r i) t -> p r t i", i=RUN)
-            raw = x_raw[:, n].rearrange("p t (r i) -> p r t i", i=RUN)
-            runs = VECTOR_PIXELS // RUN
-            nc.vector.tensor_copy(out=grouped[:, :runs], in_=raw[:, :runs])
-            nc.scalar.copy(out=grouped[:, runs:], in_=raw[:, runs:])
-
-        def quantise_image(n):
-            nc.vector.quantize_mx(
-                out=x_codes[:, n, :].bitcast(FP8X4),
-                scales=x_scales[:, n, :],
-                in_=x_grouped[:, n].rearrange("p s t -> p (s t)"),
+        def regroup(engine_copy, n, first, end):
+            engine_copy(
+                out=x_grouped[:, n, first:end, :],
+                in_=x_raw[:, n, :, first:end].rearrange("p t s -> p s t"),
             )
 
-        regroup_image(0)
-        regroup_image(1)
-        quantise_image(0)
-        quantise_image(1)
+        def regroup_v(n, first, end):
+            regroup(nc.vector.tensor_copy, n, first, end)
 
-        nc.scalar.mul(out=w_grouped[:], in_=w_t[:].rearrange("p t o -> p o t"), mul=1.0 / LAYERS)
-        bias_mean = keep.tile([P, 1], F32)
-        nc.scalar.mul(out=bias_mean[:], in_=bias_sum[:], mul=1.0 / LAYERS)
-        regroup_image(2)
-        nc.vector.quantize_mx(
-            out=w_codes[:].bitcast(FP8X4),
-            scales=w_scales[:],
-            in_=w_grouped[:].rearrange("p o t -> p (o t)"),
-        )
+        def regroup_s(n, first, end):
+            regroup(nc.scalar.copy, n, first, end)
 
-        regroup_image(3)
-        quantise_image(2)
-        quantise_image(3)
+        def quantise_pixels(n, first, end):
+            nc.vector.quantize_mx(
+                out=x_codes[:, n, first:end].bitcast(FP8X4),
+                scales=x_scales[:, n, first:end],
+                in_=x_grouped[:, n, first:end, :].rearrange("p s t -> p (s t)"),
+            )
 
-        for n in range(B):
-            y_ps = psum.tile([P, PIXELS], F32, name="y_ps%d" % n)
+        def mean_weights():
+            nc.scalar.mul(out=w_grouped[:], in_=w_t[:].rearrange("p t o -> p o t"), mul=1.0 / LAYERS)
+
+        def mean_bias():
+            nc.scalar.mul(out=bias_mean[:], in_=bias_sum[:], mul=1.0 / LAYERS)
+
+        def quantise_weights():
+            nc.vector.quantize_mx(
+                out=w_codes[:].bitcast(FP8X4),
+                scales=w_scales[:],
+                in_=w_grouped[:].rearrange("p o t -> p (o t)"),
+            )
+
+        def multiply(n, first, end):
+            y_ps[(n, first)] = psum.tile([P, end - first], F32, name="y_ps%d_%d" % (n, first))
             nc.tensor.matmul_mx(
-                out=y_ps[:],
+                out=y_ps[(n, first)][:],
                 lhsT=w_codes[:].bitcast(FP8X4),
                 lhsT_scale=w_scales[:],
-                rhs=x_codes[:, n, :].bitcast(FP8X4),
-                rhs_scale=x_scales[:, n, :],
+                rhs=x_codes[:, n, first:end].bitcast(FP8X4),
+                rhs_scale=x_scales[:, n, first:end],
                 start=True,
                 stop=True,
             )
-            if n % 2 == 0:
-                nc.scalar.activation(
-                    out=y_sb[:, n, :], in_=y_ps[:], func=IDENTITY, bias=bias_mean[:], scale=1.0
-                )
-            else:
-                nc.vector.tensor_scalar_add(out=y_sb[:, n, :], in0=y_ps[:], scalar1=bias_mean[:])
-            nc.sync.dma_start(out=out[n].rearrange("o h w -> o (h w)"), in_=y_sb[:, n, :])
+
+        def store(n, first, end):
+            nc.sync.dma_start(
+                out=out[n].rearrange("o h w -> o (h w)")[:, first:end], in_=y_sb[:, n, first:end]
+            )
+
+        def finish_s(n, first, end):
+            nc.scalar.activation(
+                out=y_sb[:, n, first:end], in_=y_ps[(n, first)][:], func=IDENTITY, bias=bias_mean[:], scale=1.0
+            )
+            store(n, first, end)
+
+        def finish_v(n, first, end):
+            nc.vector.tensor_scalar_add(out=y_sb[:, n, first:end], in0=y_ps[(n, first)][:], scalar1=bias_mean[:])
+            store(n, first, end)
+
+        load_layers(0, 1)
+        for j in range(1, TERMS):
+            load_layers(2 * j - 1, 2 * j + 1)
+        for n in range(B):
+            load_image(n)
+
+        make_identity(nc, ident[:])
+        nc.vector.memset(bias_rows[:], 0.0)
+        nc.gpsimd.dma_start(out=bias_rows[0:LAYERS, :], in_=biases)
+        nc.vector.memset(ones[:], 1.0)
+        idle_transposes(WARM)
+
+        cast_layer(0, 0)
+        transpose_term(0)
+        for j in range(1, TERMS):
+            add_layers(j, 2 * j - 1)
+            transpose_term(j)
+        nc.tensor.matmul(out=bias_sum[:], lhsT=bias_rows[:], rhs=ones[:], start=True, stop=True)
+
+        HALF = PIXELS // 2
+        regroup_s(0, 128, PIXELS)
+        regroup_v(0, 0, 128)
+        regroup_s(1, 128, PIXELS)
+        regroup_v(1, 0, 128)
+        quantise_pixels(0, 0, PIXELS)
+        mean_weights()
+        mean_bias()
+        regroup_s(2, 160, PIXELS)
+        regroup_v(2, 0, 160)
+        quantise_pixels(1, 0, PIXELS)
+        quantise_weights()
+        regroup_s(3, 208, PIXELS)
+        regroup_v(3, 0, 208)
+        multiply(0, 0, PIXELS)
+        multiply(1, 0, PIXELS)
+        quantise_pixels(2, 0, PIXELS)
+        quantise_pixels(3, 0, HALF)
+        quantise_pixels(3, HALF, PIXELS)
+        finish_s(0, 0, PIXELS)
+        finish_s(1, 0, PIXELS)
+        multiply(2, 0, PIXELS)
+        multiply(3, 0, HALF)
+        multiply(3, HALF, PIXELS)
+        finish_s(2, 0, PIXELS)
+        finish_s(3, 0, HALF)
+        finish_v(3, HALF, PIXELS)

@@ -164,17 +164,16 @@ def tile_conv_1x1_9_layer_s_kernel(tc, x, weights, biases, out):
         HALF = PIXELS // 2
         regroup_s(0, 128, PIXELS)
         regroup_v(0, 0, 128)
-        regroup_s(1, 128, PIXELS)
-        regroup_v(1, 0, 128)
-        quantise_pixels(0, 0, PIXELS)
         mean_weights()
         mean_bias()
-        regroup_s(2, 160, PIXELS)
-        regroup_v(2, 0, 160)
+        regroup_v(1, 0, PIXELS)
+        quantise_pixels(0, 0, PIXELS)
+        regroup_s(2, 128, PIXELS)
+        regroup_v(2, 0, 128)
         quantise_pixels(1, 0, PIXELS)
         quantise_weights()
-        regroup_s(3, 208, PIXELS)
-        regroup_v(3, 0, 208)
+        regroup_s(3, 192, PIXELS)
+        regroup_v(3, 0, 192)
         multiply(0, 0, PIXELS)
         multiply(1, 0, PIXELS)
         quantise_pixels(2, 0, PIXELS)

@@ -145,12 +145,13 @@ def tile_conv_1x1_9_layer_s_kernel(tc, x, weights, biases, out):
         load_layers(0, 1)
         for j in range(1, TERMS):
             load_layers(2 * j - 1, 2 * j + 1)
+        nc.gpsimd.memset(bias_rows[:], 0.0)
+        nc.sync.dma_start(out=bias_rows[0:8, :], in_=biases[0:8, :])
+        nc.sync.dma_start(out=bias_rows[8:9, :], in_=biases[8:9, :])
         for n in range(B):
             load_image(n)
 
         make_identity(nc, ident[:])
-        nc.vector.memset(bias_rows[:], 0.0)
-        nc.gpsimd.dma_start(out=bias_rows[0:LAYERS, :], in_=biases)
         nc.vector.memset(ones[:], 1.0)
         idle_transposes(WARM)
 

@@ -18,7 +18,6 @@ assert CIN == P * PACK and COUT == P
 FLOPS = 2 * B * PIXELS * CIN * COUT
 
 TERMS = 5
-WARM = 12
 
 
 def tile_conv_1x1_9_layer_s_kernel(tc, x, weights, biases, out):
@@ -45,7 +44,6 @@ def tile_conv_1x1_9_layer_s_kernel(tc, x, weights, biases, out):
         ones = keep.tile([P, 1], BF16)
         bias_sum = psum.tile([P, 1], F32)
         bias_mean = keep.tile([P, 1], F32)
-        warm = psum.tile([P, P], F32)
         y_ps = {}
         passes = []
 
@@ -60,10 +58,6 @@ def tile_conv_1x1_9_layer_s_kernel(tc, x, weights, biases, out):
                 out=x_raw[:, n].rearrange("p t s -> p (t s)"),
                 in_=x[n].rearrange("(p t) h w -> p (t h w)", t=PACK),
             )
-
-        def idle_transposes(count):
-            for k in range(count):
-                nc.tensor.matmul(out=warm[:], lhsT=ident[:], rhs=ident[:], is_transpose=True, start=True, stop=True)
 
         def cast_layer(j, i):
             nc.scalar.copy(out=term[:, j], in_=w_by_t[:, i])
@@ -153,7 +147,6 @@ def tile_conv_1x1_9_layer_s_kernel(tc, x, weights, biases, out):
 
         make_identity(nc, ident[:])
         nc.vector.memset(ones[:], 1.0)
-        idle_transposes(WARM)
 
         cast_layer(0, 0)
         transpose_term(0)

@@ -60,7 +60,7 @@ def tile_conv_1x1_9_layer_s_kernel(tc, x, weights, biases, out):
             )
 
         def cast_layer(j, i):
-            nc.scalar.copy(out=term[:, j], in_=w_by_t[:, i])
+            nc.vector.tensor_copy(out=term[:, j], in_=w_by_t[:, i])
 
         def add_layers(j, i):
             nc.vector.tensor_add(out=term[:, j], in0=w_by_t[:, i], in1=w_by_t[:, i + 1])

@@ -139,11 +139,11 @@ def tile_conv_1x1_9_layer_s_kernel(tc, x, weights, biases, out):
         load_layers(0, 1)
         for j in range(1, TERMS):
             load_layers(2 * j - 1, 2 * j + 1)
-        nc.gpsimd.memset(bias_rows[:], 0.0)
-        nc.sync.dma_start(out=bias_rows[0:8, :], in_=biases[0:8, :])
-        nc.sync.dma_start(out=bias_rows[8:9, :], in_=biases[8:9, :])
         for n in range(B):
             load_image(n)
+        nc.gpsimd.memset(bias_rows[:], 0.0)
+        nc.scalar.dma_start(out=bias_rows[0:8, :], in_=biases[0:8, :])
+        nc.scalar.dma_start(out=bias_rows[8:9, :], in_=biases[8:9, :])
 
         make_identity(nc, ident[:])
         nc.vector.memset(ones[:], 1.0)
@@ -158,16 +158,17 @@ def tile_conv_1x1_9_layer_s_kernel(tc, x, weights, biases, out):
         HALF = PIXELS // 2
         regroup_s(0, 128, PIXELS)
         regroup_v(0, 0, 128)
+        regroup_s(1, 160, PIXELS)
+        regroup_v(1, 0, 160)
         mean_weights()
         mean_bias()
-        regroup_v(1, 0, PIXELS)
         quantise_pixels(0, 0, PIXELS)
-        regroup_s(2, 128, PIXELS)
-        regroup_v(2, 0, 128)
+        regroup_s(2, 160, PIXELS)
+        regroup_v(2, 0, 160)
         quantise_pixels(1, 0, PIXELS)
         quantise_weights()
-        regroup_s(3, 192, PIXELS)
-        regroup_v(3, 0, 192)
+        regroup_s(3, 176, PIXELS)
+        regroup_v(3, 0, 176)
         multiply(0, 0, PIXELS)
         multiply(1, 0, PIXELS)
         quantise_pixels(2, 0, PIXELS)

@@ -172,13 +172,10 @@ def tile_conv_1x1_9_layer_s_kernel(tc, x, weights, biases, out):
         multiply(0, 0, PIXELS)
         multiply(1, 0, PIXELS)
         quantise_pixels(2, 0, PIXELS)
-        quantise_pixels(3, 0, HALF)
-        quantise_pixels(3, HALF, PIXELS)
+        quantise_pixels(3, 0, PIXELS)
         finish_s(0, 0, PIXELS)
         finish_s(1, 0, PIXELS)
         multiply(2, 0, PIXELS)
-        multiply(3, 0, HALF)
-        multiply(3, HALF, PIXELS)
+        multiply(3, 0, PIXELS)
         finish_s(2, 0, PIXELS)
-        finish_s(3, 0, HALF)
-        finish_v(3, HALF, PIXELS)
+        finish_v(3, 0, PIXELS)

from contextlib import ExitStack

import concourse.mybir as mybir
from concourse.masks import make_identity

BF16 = mybir.dt.bfloat16
F32 = mybir.dt.float32
U32 = mybir.dt.uint32
U8 = mybir.dt.uint8
FP8X4 = mybir.dt.float8_e4m3fn_x4
IDENTITY = mybir.ActivationFunctionType.Identity

P = 128
PACK = 4
B, CIN, PIXELS, COUT, LAYERS = 4, 512, 256, 128, 9
assert CIN == P * PACK and COUT == P

FLOPS = 2 * B * PIXELS * CIN * COUT

TERMS = 5


def tile_conv_1x1_9_layer_s_kernel(tc, x, weights, biases, out):
    nc = tc.nc
    with ExitStack() as ctx:
        keep = ctx.enter_context(tc.tile_pool(name="keep", bufs=1))
        psum = ctx.enter_context(tc.psum_pool(name="psum", bufs=1))
        ctx.enter_context(tc.manual_schedule())

        w_raw = keep.tile([P, LAYERS, CIN], BF16)
        w_by_t = w_raw[:].rearrange("o i (p t) -> o i t p", t=PACK)
        term = keep.tile([P, TERMS, PACK, P], F32)
        w_t = psum.tile([P, PACK, COUT], F32)
        w_grouped = keep.tile([P, COUT, PACK], BF16, align_bytes=64)
        w_codes = keep.tile([P, COUT], U32, align_bytes=64)
        w_scales = keep.tile([P, COUT], U8, align_bytes=64)
        x_raw = keep.tile([P, B, PACK, PIXELS], BF16)
        x_grouped = keep.tile([P, B, PIXELS, PACK], BF16, align_bytes=64)
        x_codes = keep.tile([P, B, PIXELS], U32, align_bytes=64)
        x_scales = keep.tile([P, B, PIXELS], U8, align_bytes=64)
        y_sb = keep.tile([P, B, PIXELS], F32)
        ident = keep.tile([P, P], F32)
        bias_rows = keep.tile([P, COUT], BF16)
        ones = keep.tile([P, 1], BF16)
        bias_sum = psum.tile([P, 1], F32)
        bias_mean = keep.tile([P, 1], F32)
        y_ps = {}
        passes = []

        def load_layers(first, end):
            nc.sync.dma_start(
                out=w_raw[:, first:end, :],
                in_=weights[first:end].rearrange("i o c a b -> o i (c a b)"),
            )

        def load_image(n):
            nc.sync.dma_start(
                out=x_raw[:, n].rearrange("p t s -> p (t s)"),
                in_=x[n].rearrange("(p t) h w -> p (t h w)", t=PACK),
            )

        def cast_layer(j, i):
            nc.vector.tensor_copy(out=term[:, j], in_=w_by_t[:, i])

        def add_layers(j, i):
            nc.vector.tensor_add(out=term[:, j], in0=w_by_t[:, i], in1=w_by_t[:, i + 1])

        def transpose_term(j):
            for t in range(PACK):
                passes.append(j)
                nc.tensor.matmul(
                    out=w_t[:, t, :],
                    lhsT=term[:, j, t, :],
                    rhs=ident[:],
                    is_transpose=True,
                    start=(len(passes) == 1),
                    stop=(len(passes) == TERMS * PACK),
                )

        def regroup(engine_copy, n, first, end):
            engine_copy(
                out=x_grouped[:, n, first:end, :],
                in_=x_raw[:, n, :, first:end].rearrange("p t s -> p s t"),
            )

        def regroup_v(n, first, end):
            regroup(nc.vector.tensor_copy, n, first, end)

        def regroup_s(n, first, end):
            regroup(nc.scalar.copy, n, first, end)

        def quantise_pixels(n, first, end):
            nc.vector.quantize_mx(
                out=x_codes[:, n, first:end].bitcast(FP8X4),
                scales=x_scales[:, n, first:end],
                in_=x_grouped[:, n, first:end, :].rearrange("p s t -> p (s t)"),
            )

        def mean_weights():
            nc.scalar.mul(out=w_grouped[:], in_=w_t[:].rearrange("p t o -> p o t"), mul=1.0 / LAYERS)

        def mean_bias():
            nc.scalar.mul(out=bias_mean[:], in_=bias_sum[:], mul=1.0 / LAYERS)

        def quantise_weights():
            nc.vector.quantize_mx(
                out=w_codes[:].bitcast(FP8X4),
                scales=w_scales[:],
                in_=w_grouped[:].rearrange("p o t -> p (o t)"),
            )

        def multiply(n, first, end):
            y_ps[(n, first)] = psum.tile([P, end - first], F32, name="y_ps%d_%d" % (n, first))
            nc.tensor.matmul_mx(
                out=y_ps[(n, first)][:],
                lhsT=w_codes[:].bitcast(FP8X4),
                lhsT_scale=w_scales[:],
                rhs=x_codes[:, n, first:end].bitcast(FP8X4),
                rhs_scale=x_scales[:, n, first:end],
                start=True,
                stop=True,
            )

        def store(n, first, end):
            nc.sync.dma_start(
                out=out[n].rearrange("o h w -> o (h w)")[:, first:end], in_=y_sb[:, n, first:end]
            )

        def finish_s(n, first, end):
            nc.scalar.activation(
                out=y_sb[:, n, first:end], in_=y_ps[(n, first)][:], func=IDENTITY, bias=bias_mean[:], scale=1.0
            )
            store(n, first, end)

        def finish_v(n, first, end):
            nc.vector.tensor_scalar_add(out=y_sb[:, n, first:end], in0=y_ps[(n, first)][:], scalar1=bias_mean[:])
            store(n, first, end)

        load_layers(0, 1)
        for j in range(1, TERMS):
            load_layers(2 * j - 1, 2 * j + 1)
        for n in range(B):
            load_image(n)
        nc.gpsimd.memset(bias_rows[:], 0.0)
        nc.scalar.dma_start(out=bias_rows[0:8, :], in_=biases[0:8, :])
        nc.scalar.dma_start(out=bias_rows[8:9, :], in_=biases[8:9, :])

        make_identity(nc, ident[:])
        nc.vector.memset(ones[:], 1.0)

        cast_layer(0, 0)
        transpose_term(0)
        for j in range(1, TERMS):
            add_layers(j, 2 * j - 1)
            transpose_term(j)
        nc.tensor.matmul(out=bias_sum[:], lhsT=bias_rows[:], rhs=ones[:], start=True, stop=True)

        HALF = PIXELS // 2
        regroup_s(0, 128, PIXELS)
        regroup_v(0, 0, 128)
        regroup_s(1, 160, PIXELS)
        regroup_v(1, 0, 160)
        mean_weights()
        mean_bias()
        quantise_pixels(0, 0, PIXELS)
        regroup_s(2, 160, PIXELS)
        regroup_v(2, 0, 160)
        quantise_pixels(1, 0, PIXELS)
        quantise_weights()
        regroup_s(3, 176, PIXELS)
        regroup_v(3, 0, 176)
        multiply(0, 0, PIXELS)
        multiply(1, 0, PIXELS)
        quantise_pixels(2, 0, PIXELS)
        quantise_pixels(3, 0, PIXELS)
        finish_s(0, 0, PIXELS)
        finish_s(1, 0, PIXELS)
        multiply(2, 0, PIXELS)
        multiply(3, 0, PIXELS)
        finish_s(2, 0, PIXELS)
        finish_v(3, 0, PIXELS)
